import numpy as np
import ml_dtypes


def mxq(x, axis, fmt="e4m3"):
    dtype, down = {"e4m3": (ml_dtypes.float8_e4m3fn, 7), "e5m2": (ml_dtypes.float8_e5m2, 14)}[fmt]
    v = np.moveaxis(np.asarray(x, np.float32).astype(ml_dtypes.bfloat16).astype(np.float64), axis, -1)
    blocks = v.reshape(v.shape[:-1] + (-1, 32))
    amax = np.abs(blocks).max(-1, keepdims=True)
    byte = np.maximum(np.where(amax > 0, np.frexp(amax)[1] - 1 + 127, 0) - down, 1)
    scale = np.exp2(byte - 127.0)
    codes = (blocks / scale).astype(np.float32).astype(dtype).astype(np.float64)
    return np.moveaxis((codes * scale).reshape(v.shape), -1, axis)


WIDE = False


def mx_kscale(k):
    if not WIDE:
        return np.ones(k)
    levels = np.array([10, -10, 5, -5, 0])
    if k % 512:
        return np.exp2(np.random.permutation(np.resize(levels, k // 32))).repeat(32)
    a = np.empty((k // 512, 16))
    for p in range(k // 512):
        a[p, :8] = np.random.permutation(np.resize(levels, 8))
        for g in range(8):
            far = levels[np.abs(levels - a[p, g]) >= 10]
            a[p, g + 8] = far[np.random.randint(len(far))]
    return np.exp2(a.ravel()).repeat(32)


BF16 = ml_dtypes.bfloat16


def bf(x):
    return np.asarray(x, np.float32).astype(BF16)


def f64(x):
    return np.asarray(x).astype(np.float64)


B, NH, T, D, N, CK = 1, 6, 1024, 512, 256, 512
THETA = 2.0 ** 16


def get_freqs(n):
    q = f64(np.repeat(np.arange(0, n, 2), 2))
    return 1.0 / (THETA ** (q / n)) / (2.0 * np.pi)


def rope(phases, v):
    ph = phases * (2.0 * np.pi)
    c, s = np.cos(ph), np.sin(ph)
    even = v[..., 0::2]
    odd = v[..., 1::2]
    v_rot = np.stack((-odd, even), axis=-1).reshape(v.shape)
    return v * c + v_rot * s


def draw0():
    s = mx_kscale(D)
    return {'x': bf(np.random.standard_normal((B, 1, T, D)) * s),
            'encoder': bf(np.random.standard_normal((NH, D, N)) * 0.5 / np.sqrt(D) / s[:, None])}


def core(x, encoder):
    x_latent = mxq(f64(x), 3, 'e4m3') @ mxq(f64(encoder), 1, 'e4m3')
    x_sparse = np.maximum(x_latent, 0.0)
    phases = f64(np.arange(T))[:, None] * get_freqs(N)[None, :]
    qr = rope(phases, x_sparse)
    return x_sparse, qr


def e4m3fn_bytes(y):
    return np.clip(np.asarray(y, np.float64), -448.0, 448.0).astype(np.float32).astype(ml_dtypes.float8_e4m3fn).view(np.uint8)


def e4m3fn_values(b):
    return np.asarray(b, np.uint8).view(ml_dtypes.float8_e4m3fn).astype(np.float64)


def setup_inputs():
    d = draw0()
    x0 = np.asarray(d['encoder']).astype(np.float64)
    s = (np.max(np.abs(x0), axis=(0, 2), keepdims=True) / 448.0).astype(np.float32)
    out = {}
    for k, v in d.items():
        if k == 'encoder':
            out['encoder_bytes'] = e4m3fn_bytes(x0 / s.astype(np.float64))
            out['encoder_scale'] = s
        else:
            out[k] = v
    return out


def reference(x, encoder_bytes, encoder_scale):
    return core(x, e4m3fn_values(encoder_bytes) * encoder_scale.astype(np.float64))

@@ -1,0 +1,192 @@
+from contextlib import ExitStack
+
+import concourse.mybir as mybir
+from concourse.masks import make_identity
+
+FLOPS = 2 * 1024 * 512 * 1536
+
+F32 = mybir.dt.float32
+BF16 = mybir.dt.bfloat16
+I32 = mybir.dt.int32
+U32 = mybir.dt.uint32
+U8 = mybir.dt.uint8
+FP8 = mybir.dt.float8_e4m3fn
+FP8X4 = mybir.dt.float8_e4m3fn_x4
+ALU = mybir.AluOpType
+ACT = mybir.ActivationFunctionType
+
+P = 128
+NH = 6
+N = 256
+NPAIR = 128
+TPP = 8
+TWO_PI = 6.283185307179586
+V_HEADS = 1
+
+
+def tile_bdhlayer_pa_kernel(tc, x, encoder_bytes, encoder_scale, out_0, out_1):
+    nc = tc.nc
+    with ExitStack() as ctx:
+        const = ctx.enter_context(tc.tile_pool(name="const", bufs=1))
+        work = ctx.enter_context(tc.tile_pool(name="work", bufs=2))
+        outp = ctx.enter_context(tc.tile_pool(name="outp", bufs=4))
+        prod = ctx.enter_context(tc.tile_pool(name="prod", bufs=3))
+        psx = ctx.enter_context(tc.psum_pool(name="psx", bufs=2))
+        psm = ctx.enter_context(tc.psum_pool(name="psm", bufs=6))
+
+        sc = const.tile([P, 4], F32, name="sc")
+        nc.sync.dma_start(out=sc[:], in_=encoder_scale.rearrange("o (p t) u -> p (o t u)", t=4))
+        eb = [const.tile([P, 4 * N], U8, name="eb%d" % h) for h in range(NH)]
+        xin = [const.tile([P, 2, 512], BF16, name="xin%d" % c) for c in range(4)]
+        xr = x.rearrange("b o (p a) k -> p (b o a) k", a=TPP)
+
+        def load_enc(h):
+            nc.sync.dma_start(out=eb[h][:], in_=encoder_bytes[h].rearrange("(p t) n -> p (t n)", t=4))
+
+        def load_x(c):
+            nc.sync.dma_start(out=xin[c][:], in_=xr[:, 2 * c:2 * c + 2, :])
+
+        load_enc(0)
+        load_x(0)
+        load_x(1)
+        load_enc(1)
+        load_x(2)
+        load_x(3)
+        for h in range(2, NH):
+            load_enc(h)
+
+        warm = const.tile([P, 1], F32, name="warm")
+        warm2 = const.tile([P, 1], F32, name="warm2")
+        nc.vector.memset(warm[:], 0.0)
+        nc.scalar.activation(out=warm2[:], in_=warm[:], func=ACT.Sin)
+
+        tcol = const.tile([P, TPP], F32, name="tcol")
+        nc.gpsimd.iota(tcol[:], pattern=[[1, TPP]], base=0, channel_multiplier=TPP,
+                       allow_small_or_imprecise_dtypes=True)
+        ident = const.tile([P, P], F32, name="ident")
+        make_identity(nc, ident[:])
+
+        g = const.tile([P, NPAIR], F32, name="g")
+        nc.vector.memset(g[:, 0:8], 1.0)
+        for m in range(8):
+            nc.vector.tensor_scalar(out=g[:, m:m + 1], in0=g[:, m:m + 1],
+                                    scalar1=2.0 ** (-m / 8.0) / TWO_PI, scalar2=None, op0=ALU.mult)
+        for b in range(4):
+            wd = 8 << b
+            nc.vector.tensor_scalar(out=g[:, wd:2 * wd], in0=g[:, 0:wd],
+                                    scalar1=2.0 ** (-(1 << b)), scalar2=None, op0=ALU.mult)
+
+        kint = const.tile([P, TPP, NPAIR], I32, name="kint")
+        frac = const.tile([P, TPP, NPAIR], F32, name="frac")
+        afr = const.tile([P, TPP, NPAIR], F32, name="afr")
+        cosT = const.tile([P, TPP, NPAIR], F32, name="cosT")
+        sinT = const.tile([P, 2, TPP, NPAIR], F32, name="sinT")
+
+        def tables_a(q):
+            a0 = 4 * q
+            for a in range(a0, a0 + 4):
+                nc.gpsimd.tensor_scalar(out=kint[:, a, :], in0=g[:], scalar1=tcol[:, a:a + 1],
+                                        scalar2=0.0, op0=ALU.mult, op1=ALU.add)
+                nc.vector.scalar_tensor_tensor(out=frac[:, a, :], in0=g[:], scalar=tcol[:, a:a + 1],
+                                               in1=kint[:, a, :], op0=ALU.mult, op1=ALU.subtract)
+            sl = slice(a0, a0 + 4)
+            nc.vector.scalar_tensor_tensor(out=afr[:, sl, :], in0=frac[:, sl, :], scalar=-1.0,
+                                           in1=frac[:, sl, :], op0=ALU.mult, op1=ALU.max)
+
+        def tables_b(q):
+            sl = slice(4 * q, 4 * q + 4)
+            nc.scalar.activation(out=sinT[:, 1, sl, :], in_=frac[:, sl, :], func=ACT.Sin, scale=TWO_PI)
+            nc.scalar.activation(out=cosT[:, sl, :], in_=afr[:, sl, :], func=ACT.Sin,
+                                 scale=-TWO_PI, bias=TWO_PI / 4.0)
+            nc.vector.tensor_scalar(out=sinT[:, 0, sl, :], in0=sinT[:, 1, sl, :], scalar1=-1.0,
+                                    scalar2=None, op0=ALU.mult)
+
+        xc = [const.tile([P, 2 * P], U32, name="xc%d" % c, align_bytes=64) for c in range(4)]
+        xs = [const.tile([P, 2 * P], U8, name="xs%d" % c, align_bytes=64) for c in range(4)]
+
+        def prep_x(c):
+            xt = psx.tile([P, 2, 2, P], F32, name="xt")
+            for j in range(2):
+                words = xin[c][:, j, :].bitcast(F32)
+                for u in range(2):
+                    nc.tensor.transpose(xt[:, j, u, :], words[:, u:256:2], ident[:])
+            xg = work.tile([P, 2 * P * 4], BF16, name="xg", align_bytes=64)
+            copier = nc.vector.tensor_copy if c == 0 else nc.scalar.copy
+            copier(out=xg[:].bitcast(F32).rearrange("p (a r u) -> p a r u", a=2, u=2),
+                   in_=xt[:].rearrange("p a u r -> p a r u"))
+            nc.vector.quantize_mx(out=xc[c][:].bitcast(FP8X4), scales=xs[c][:], in_=xg[:])
+
+        ec = [const.tile([P, N], U32, name="ec%d" % h, align_bytes=64) for h in range(NH)]
+        es = [const.tile([P, N], U8, name="es%d" % h, align_bytes=64) for h in range(NH)]
+
+        def prep_enc(h):
+            eg = work.tile([P, N, 4], BF16, name="eg", align_bytes=64)
+            if h < V_HEADS:
+                for t in range(4):
+                    nc.vector.tensor_scalar(out=eg[:, :, t], in0=eb[h][:, t * N:(t + 1) * N].bitcast(FP8),
+                                            scalar1=sc[:, t:t + 1], scalar2=None, op0=ALU.mult)
+            else:
+                ew = work.tile([P, 4, N], BF16, name="ew")
+                for t in range(4):
+                    nc.scalar.activation(out=ew[:, t, :], in_=eb[h][:, t * N:(t + 1) * N].bitcast(FP8),
+                                         func=ACT.Copy, scale=sc[:, t:t + 1])
+                nc.scalar.copy(out=eg[:], in_=ew[:].rearrange("p t n -> p n t"))
+            nc.vector.quantize_mx(out=ec[h][:].bitcast(FP8X4), scales=es[h][:],
+                                  in_=eg[:].rearrange("p n t -> p (n t)"))
+
+        tables_a(0)
+        tables_a(1)
+        tables_b(0)
+        prep_enc(0)
+        prep_x(0)
+        tables_b(1)
+        prep_x(1)
+        prep_x(2)
+        prep_x(3)
+        prep_enc(1)
+
+        for h in range(NH):
+            o0 = out_0[0, h].rearrange("(p a) n -> p (a n)", a=TPP)
+            o1 = out_1[0, h].rearrange("(p a) n -> p (a n)", a=TPP)
+            per_store = 1 if h == NH - 1 else 2
+            for c in range(4):
+                cc = c % per_store
+                if cc == 0:
+                    xsp = outp.tile([P, per_store * 2 * N], F32, name="xsp")
+                    qrt = outp.tile([P, per_store * 2 * N], F32, name="qrt")
+                ps = psm.tile([P, 2, N], F32, name="ps")
+                for j in range(2):
+                    nc.tensor.matmul_mx(out=ps[:, j, :],
+                                        lhsT=xc[c][:, j * P:(j + 1) * P].bitcast(FP8X4),
+                                        lhsT_scale=xs[c][:, j * P:(j + 1) * P],
+                                        rhs=ec[h][:].bitcast(FP8X4), rhs_scale=es[h][:],
+                                        start=True, stop=True)
+                c0 = cc * 2 * N
+                nc.scalar.activation(out=xsp[:, c0:c0 + 2 * N], in_=ps[:].rearrange("p a n -> p (a n)"),
+                                     func=ACT.Relu)
+                pairs = ps[:].rearrange("p a (i e) -> p (a i) e", e=2)
+                u = prod.tile([P, 2 * NPAIR, 2], F32, name="u")
+                w = prod.tile([P, 2 * NPAIR, 2], F32, name="w")
+                asl = slice(2 * c, 2 * c + 2)
+                nc.vector.scalar_tensor_tensor(
+                    out=u[:], in0=pairs, scalar=0.0,
+                    in1=cosT[:, asl, :].rearrange("p a i -> p (a i)").unsqueeze(2).to_broadcast([P, 2 * NPAIR, 2]),
+                    op0=ALU.max, op1=ALU.mult)
+                nc.vector.scalar_tensor_tensor(
+                    out=w[:], in0=pairs[:, :, ::-1], scalar=0.0,
+                    in1=sinT[:, :, asl, :].rearrange("p e a i -> p (a i) e"),
+                    op0=ALU.max, op1=ALU.mult)
+                uf = u[:].rearrange("p j e -> p (j e)")
+                wf = w[:].rearrange("p j e -> p (j e)")
+                if h == NH - 1 and c == 3:
+                    nc.gpsimd.tensor_tensor(out=qrt[:, c0:c0 + N], in0=uf[:, 0:N], in1=wf[:, 0:N], op=ALU.add)
+                    nc.vector.tensor_tensor(out=qrt[:, c0 + N:c0 + 2 * N], in0=uf[:, N:2 * N],
+                                            in1=wf[:, N:2 * N], op=ALU.add)
+                else:
+                    nc.gpsimd.tensor_tensor(out=qrt[:, c0:c0 + 2 * N], in0=uf, in1=wf, op=ALU.add)
+                if cc == per_store - 1:
+                    hc = slice((c - cc) * 2 * N, (c + 1) * 2 * N)
+                    nc.sync.dma_start(out=o0[:, hc], in_=xsp[:])
+                    nc.sync.dma_start(out=o1[:, hc], in_=qrt[:])
+                if c == 1 and h + 2 < NH:
+                    prep_enc(h + 2)

@@ -21,7 +21,7 @@ N = 256
 NPAIR = 128
 TPP = 8
 TWO_PI = 6.283185307179586
-V_HEADS = 1
+ENC_GROUPS = ((0,), (1,), (2,), (3,), (4, 5))
 
 
 def tile_bdhlayer_pa_kernel(tc, x, encoder_bytes, encoder_scale, out_0, out_1):
@@ -31,17 +31,18 @@ def tile_bdhlayer_pa_kernel(tc, x, encoder_bytes, encoder_scale, out_0, out_1):
         work = ctx.enter_context(tc.tile_pool(name="work", bufs=2))
         outp = ctx.enter_context(tc.tile_pool(name="outp", bufs=4))
         prod = ctx.enter_context(tc.tile_pool(name="prod", bufs=3))
-        psx = ctx.enter_context(tc.psum_pool(name="psx", bufs=2))
-        psm = ctx.enter_context(tc.psum_pool(name="psm", bufs=6))
+        psm = ctx.enter_context(tc.psum_pool(name="psm", bufs=8))
 
         sc = const.tile([P, 4], F32, name="sc")
         nc.sync.dma_start(out=sc[:], in_=encoder_scale.rearrange("o (p t) u -> p (o t u)", t=4))
-        eb = [const.tile([P, 4 * N], U8, name="eb%d" % h) for h in range(NH)]
+        eb = [const.tile([P, 4, len(grp), N], U8, name="eb%d" % gi) for gi, grp in enumerate(ENC_GROUPS)]
         xin = [const.tile([P, 2, 512], BF16, name="xin%d" % c) for c in range(4)]
         xr = x.rearrange("b o (p a) k -> p (b o a) k", a=TPP)
 
-        def load_enc(h):
-            nc.sync.dma_start(out=eb[h][:], in_=encoder_bytes[h].rearrange("(p t) n -> p (t n)", t=4))
+        def load_enc(gi):
+            for s, h in enumerate(ENC_GROUPS[gi]):
+                nc.sync.dma_start(out=eb[gi][:, :, s, :],
+                                  in_=encoder_bytes[h].rearrange("(p t) n -> p t n", t=4))
 
         def load_x(c):
             nc.sync.dma_start(out=xin[c][:], in_=xr[:, 2 * c:2 * c + 2, :])
@@ -52,8 +53,9 @@ def tile_bdhlayer_pa_kernel(tc, x, encoder_bytes, encoder_scale, out_0, out_1):
         load_enc(1)
         load_x(2)
         load_x(3)
-        for h in range(2, NH):
-            load_enc(h)
+        load_enc(2)
+        load_enc(3)
+        load_enc(4)
 
         warm = const.tile([P, 1], F32, name="warm")
         warm2 = const.tile([P, 1], F32, name="warm2")
@@ -67,14 +69,12 @@ def tile_bdhlayer_pa_kernel(tc, x, encoder_bytes, encoder_scale, out_0, out_1):
         make_identity(nc, ident[:])
 
         g = const.tile([P, NPAIR], F32, name="g")
-        nc.vector.memset(g[:, 0:8], 1.0)
-        for m in range(8):
-            nc.vector.tensor_scalar(out=g[:, m:m + 1], in0=g[:, m:m + 1],
-                                    scalar1=2.0 ** (-m / 8.0) / TWO_PI, scalar2=None, op0=ALU.mult)
-        for b in range(4):
-            wd = 8 << b
+        nc.vector.memset(g[:, 0:1], 1.0)
+        nc.vector.tensor_scalar(out=g[:, 0:1], in0=g[:, 0:1], scalar1=1.0 / TWO_PI, scalar2=None, op0=ALU.mult)
+        for b in range(7):
+            wd = 1 << b
             nc.vector.tensor_scalar(out=g[:, wd:2 * wd], in0=g[:, 0:wd],
-                                    scalar1=2.0 ** (-(1 << b)), scalar2=None, op0=ALU.mult)
+                                    scalar1=2.0 ** (-wd / 8.0), scalar2=None, op0=ALU.mult)
 
         kint = const.tile([P, TPP, NPAIR], I32, name="kint")
         frac = const.tile([P, TPP, NPAIR], F32, name="frac")
@@ -82,111 +82,184 @@ def tile_bdhlayer_pa_kernel(tc, x, encoder_bytes, encoder_scale, out_0, out_1):
         cosT = const.tile([P, TPP, NPAIR], F32, name="cosT")
         sinT = const.tile([P, 2, TPP, NPAIR], F32, name="sinT")
 
-        def tables_a(q):
-            a0 = 4 * q
-            for a in range(a0, a0 + 4):
-                nc.gpsimd.tensor_scalar(out=kint[:, a, :], in0=g[:], scalar1=tcol[:, a:a + 1],
-                                        scalar2=0.0, op0=ALU.mult, op1=ALU.add)
-                nc.vector.scalar_tensor_tensor(out=frac[:, a, :], in0=g[:], scalar=tcol[:, a:a + 1],
-                                               in1=kint[:, a, :], op0=ALU.mult, op1=ALU.subtract)
-            sl = slice(a0, a0 + 4)
-            nc.vector.scalar_tensor_tensor(out=afr[:, sl, :], in0=frac[:, sl, :], scalar=-1.0,
-                                           in1=frac[:, sl, :], op0=ALU.mult, op1=ALU.max)
+        def table_k(a, eng):
+            eng.tensor_scalar(out=kint[:, a, :], in0=g[:], scalar1=tcol[:, a:a + 1],
+                              scalar2=0.0, op0=ALU.mult, op1=ALU.add)
 
-        def tables_b(q):
-            sl = slice(4 * q, 4 * q + 4)
+        def table_frac(a):
+            nc.vector.scalar_tensor_tensor(out=frac[:, a, :], in0=g[:], scalar=tcol[:, a:a + 1],
+                                           in1=kint[:, a, :], op0=ALU.mult, op1=ALU.subtract)
+
+        def table_trig(a0, a1, neg_on_scalar):
+            sl = slice(a0, a1)
             nc.scalar.activation(out=sinT[:, 1, sl, :], in_=frac[:, sl, :], func=ACT.Sin, scale=TWO_PI)
+            if neg_on_scalar:
+                nc.scalar.activation(out=sinT[:, 0, sl, :], in_=frac[:, sl, :], func=ACT.Sin, scale=-TWO_PI)
+            nc.scalar.activation(out=afr[:, sl, :], in_=frac[:, sl, :], func=ACT.Abs)
             nc.scalar.activation(out=cosT[:, sl, :], in_=afr[:, sl, :], func=ACT.Sin,
                                  scale=-TWO_PI, bias=TWO_PI / 4.0)
-            nc.vector.tensor_scalar(out=sinT[:, 0, sl, :], in0=sinT[:, 1, sl, :], scalar1=-1.0,
-                                    scalar2=None, op0=ALU.mult)
+            if not neg_on_scalar:
+                nc.gpsimd.tensor_scalar(out=sinT[:, 0, sl, :], in0=sinT[:, 1, sl, :], scalar1=-1.0,
+                                        scalar2=0.0, op0=ALU.mult, op1=ALU.add)
 
-        xc = [const.tile([P, 2 * P], U32, name="xc%d" % c, align_bytes=64) for c in range(4)]
-        xs = [const.tile([P, 2 * P], U8, name="xs%d" % c, align_bytes=64) for c in range(4)]
+        xc = const.tile([P, TPP * P], U32, name="xc", align_bytes=64)
+        xs = const.tile([P, TPP * P], U8, name="xs", align_bytes=64)
 
-        def prep_x(c):
-            xt = psx.tile([P, 2, 2, P], F32, name="xt")
+        xg = [None, None, None, None]
+
+        def x_transpose(c, tile_, col0):
+            xt = psm.tile([P, 2, 2, P], F32, name="ps")
             for j in range(2):
                 words = xin[c][:, j, :].bitcast(F32)
                 for u in range(2):
                     nc.tensor.transpose(xt[:, j, u, :], words[:, u:256:2], ident[:])
-            xg = work.tile([P, 2 * P * 4], BF16, name="xg", align_bytes=64)
-            copier = nc.vector.tensor_copy if c == 0 else nc.scalar.copy
-            copier(out=xg[:].bitcast(F32).rearrange("p (a r u) -> p a r u", a=2, u=2),
+            xg[c] = (xt, tile_, col0)
+
+        def x_copy(c, copier):
+            xt, tile_, col0 = xg[c]
+            copier(out=tile_[:, col0:col0 + 1024].bitcast(F32).rearrange("p (a r u) -> p a r u", a=2, u=2),
                    in_=xt[:].rearrange("p a u r -> p a r u"))
-            nc.vector.quantize_mx(out=xc[c][:].bitcast(FP8X4), scales=xs[c][:], in_=xg[:])
 
-        ec = [const.tile([P, N], U32, name="ec%d" % h, align_bytes=64) for h in range(NH)]
-        es = [const.tile([P, N], U8, name="es%d" % h, align_bytes=64) for h in range(NH)]
+        def x_quant(c0, c1, tile_):
+            cols = slice(c0 * 2 * P, c1 * 2 * P)
+            nc.vector.quantize_mx(out=xc[:, cols].bitcast(FP8X4), scales=xs[:, cols], in_=tile_[:])
 
-        def prep_enc(h):
-            eg = work.tile([P, N, 4], BF16, name="eg", align_bytes=64)
-            if h < V_HEADS:
-                for t in range(4):
-                    nc.vector.tensor_scalar(out=eg[:, :, t], in0=eb[h][:, t * N:(t + 1) * N].bitcast(FP8),
+        ec = [const.tile([P, len(grp) * N], U32, name="ec%d" % gi, align_bytes=64) for gi, grp in enumerate(ENC_GROUPS)]
+        es = [const.tile([P, len(grp) * N], U8, name="es%d" % gi, align_bytes=64) for gi, grp in enumerate(ENC_GROUPS)]
+        where = {}
+        for gi, grp in enumerate(ENC_GROUPS):
+            for s, h in enumerate(grp):
+                where[h] = (gi, s)
+
+        def enc_pieces(gi):
+            wdt = len(ENC_GROUPS[gi]) * N
+            src = eb[gi][:].rearrange("p t s n -> p t (s n)")
+            t_ = {}
+
+            def widen(t):
+                if t == 0:
+                    t_["eg"] = work.tile([P, wdt, 4], BF16, name="eg%d" % wdt, align_bytes=64)
+                    if gi > 0:
+                        t_["ew"] = work.tile([P, 4, wdt], BF16, name="ew%d" % wdt)
+                if gi == 0:
+                    nc.vector.tensor_scalar(out=t_["eg"][:, :, t], in0=src[:, t, :].bitcast(FP8),
                                             scalar1=sc[:, t:t + 1], scalar2=None, op0=ALU.mult)
-            else:
-                ew = work.tile([P, 4, N], BF16, name="ew")
-                for t in range(4):
-                    nc.scalar.activation(out=ew[:, t, :], in_=eb[h][:, t * N:(t + 1) * N].bitcast(FP8),
+                else:
+                    nc.scalar.activation(out=t_["ew"][:, t, :], in_=src[:, t, :].bitcast(FP8),
                                          func=ACT.Copy, scale=sc[:, t:t + 1])
-                nc.scalar.copy(out=eg[:], in_=ew[:].rearrange("p t n -> p n t"))
-            nc.vector.quantize_mx(out=ec[h][:].bitcast(FP8X4), scales=es[h][:],
-                                  in_=eg[:].rearrange("p n t -> p (n t)"))
 
-        tables_a(0)
-        tables_a(1)
-        tables_b(0)
-        prep_enc(0)
-        prep_x(0)
-        tables_b(1)
-        prep_x(1)
-        prep_x(2)
-        prep_x(3)
-        prep_enc(1)
+            def interleave(n0):
+                nc.scalar.copy(out=t_["eg"][:, n0:n0 + 128, :],
+                               in_=t_["ew"][:, :, n0:n0 + 128].rearrange("p t n -> p n t"))
 
-        for h in range(NH):
+            def quantize():
+                nc.vector.quantize_mx(out=ec[gi][:].bitcast(FP8X4), scales=es[gi][:],
+                                      in_=t_["eg"][:].rearrange("p n t -> p (n t)"))
+
+            steps = [lambda t=t: widen(t) for t in range(4)]
+            if gi > 0:
+                steps.extend([lambda n0=n0: interleave(n0) for n0 in range(0, wdt, 128)])
+            steps.append(quantize)
+            return steps
+
+        def prep_enc(gi):
+            for step in enc_pieces(gi):
+                step()
+
+
+        xga = work.tile([P, 1024], BF16, name="xga", align_bytes=64)
+        xgb = work.tile([P, 1024], BF16, name="xgb", align_bytes=64)
+        xgc = work.tile([P, 2048], BF16, name="xgc", align_bytes=64)
+
+        banks = {}
+
+        def mm(b):
+            h, c = divmod(b, 4)
+            gi, s = where[h]
+            ps = psm.tile([P, 2, N], F32, name="ps")
+            for j in range(2):
+                tok = slice((2 * c + j) * P, (2 * c + j + 1) * P)
+                nc.tensor.matmul_mx(out=ps[:, j, :],
+                                    lhsT=xc[:, tok].bitcast(FP8X4), lhsT_scale=xs[:, tok],
+                                    rhs=ec[gi][:, s * N:(s + 1) * N].bitcast(FP8X4),
+                                    rhs_scale=es[gi][:, s * N:(s + 1) * N],
+                                    start=True, stop=True)
+            banks[b] = ps
+
+        for a in range(2):
+            table_k(a, nc.vector)
+            table_frac(a)
+        for a in range(2, TPP):
+            table_k(a, nc.gpsimd)
+        table_trig(0, 2, True)
+        table_frac(2)
+        table_frac(3)
+        table_trig(2, 4, False)
+        e0 = enc_pieces(0)
+        for step in e0[:4]:
+            step()
+        x_transpose(0, xga, 0)
+        x_copy(0, nc.vector.tensor_copy)
+        for a in range(4, TPP):
+            table_frac(a)
+        e0[4]()
+        x_quant(0, 1, xga)
+        x_transpose(1, xgb, 0)
+        x_transpose(2, xgc, 0)
+        x_transpose(3, xgc, 1024)
+        x_copy(1, nc.scalar.copy)
+        mm(0)
+        x_quant(1, 2, xgb)
+        mm(1)
+        x_copy(2, nc.scalar.copy)
+        x_copy(3, nc.scalar.copy)
+        table_trig(4, TPP, False)
+
+        todo = []
+        for gi in range(1, len(ENC_GROUPS)):
+            todo.extend(enc_pieces(gi))
+        PER_BANK = (3, 3, 1, 2, 2, 2, 1, 2, 2, 2, 1, 3, 2, 2, 2) + (0,) * 9
+
+        outs = {}
+        for b in range(4 * NH):
+            h, c = divmod(b, 4)
             o0 = out_0[0, h].rearrange("(p a) n -> p (a n)", a=TPP)
             o1 = out_1[0, h].rearrange("(p a) n -> p (a n)", a=TPP)
-            per_store = 1 if h == NH - 1 else 2
-            for c in range(4):
-                cc = c % per_store
-                if cc == 0:
-                    xsp = outp.tile([P, per_store * 2 * N], F32, name="xsp")
-                    qrt = outp.tile([P, per_store * 2 * N], F32, name="qrt")
-                ps = psm.tile([P, 2, N], F32, name="ps")
-                for j in range(2):
-                    nc.tensor.matmul_mx(out=ps[:, j, :],
-                                        lhsT=xc[c][:, j * P:(j + 1) * P].bitcast(FP8X4),
-                                        lhsT_scale=xs[c][:, j * P:(j + 1) * P],
-                                        rhs=ec[h][:].bitcast(FP8X4), rhs_scale=es[h][:],
-                                        start=True, stop=True)
-                c0 = cc * 2 * N
-                nc.scalar.activation(out=xsp[:, c0:c0 + 2 * N], in_=ps[:].rearrange("p a n -> p (a n)"),
-                                     func=ACT.Relu)
-                pairs = ps[:].rearrange("p a (i e) -> p (a i) e", e=2)
-                u = prod.tile([P, 2 * NPAIR, 2], F32, name="u")
-                w = prod.tile([P, 2 * NPAIR, 2], F32, name="w")
-                asl = slice(2 * c, 2 * c + 2)
-                nc.vector.scalar_tensor_tensor(
-                    out=u[:], in0=pairs, scalar=0.0,
-                    in1=cosT[:, asl, :].rearrange("p a i -> p (a i)").unsqueeze(2).to_broadcast([P, 2 * NPAIR, 2]),
-                    op0=ALU.max, op1=ALU.mult)
-                nc.vector.scalar_tensor_tensor(
-                    out=w[:], in0=pairs[:, :, ::-1], scalar=0.0,
-                    in1=sinT[:, :, asl, :].rearrange("p e a i -> p (a i) e"),
-                    op0=ALU.max, op1=ALU.mult)
-                uf = u[:].rearrange("p j e -> p (j e)")
-                wf = w[:].rearrange("p j e -> p (j e)")
-                if h == NH - 1 and c == 3:
-                    nc.gpsimd.tensor_tensor(out=qrt[:, c0:c0 + N], in0=uf[:, 0:N], in1=wf[:, 0:N], op=ALU.add)
-                    nc.vector.tensor_tensor(out=qrt[:, c0 + N:c0 + 2 * N], in0=uf[:, N:2 * N],
-                                            in1=wf[:, N:2 * N], op=ALU.add)
-                else:
-                    nc.gpsimd.tensor_tensor(out=qrt[:, c0:c0 + 2 * N], in0=uf, in1=wf, op=ALU.add)
-                if cc == per_store - 1:
-                    hc = slice((c - cc) * 2 * N, (c + 1) * 2 * N)
-                    nc.sync.dma_start(out=o0[:, hc], in_=xsp[:])
-                    nc.sync.dma_start(out=o1[:, hc], in_=qrt[:])
-                if c == 1 and h + 2 < NH:
-                    prep_enc(h + 2)
+            alone = b < 2 or b >= 4 * NH - 4
+            cc = c % 2
+            if cc == 0:
+                xsp = outp.tile([P, 4 * N], F32, name="xsp")
+                qrt = outp.tile([P, 4 * N], F32, name="qrt")
+                u = prod.tile([P, 4 * N], F32, name="u")
+                w = prod.tile([P, 4 * N], F32, name="w")
+            ps = banks[b]
+            cols = slice(cc * 2 * N, (cc + 1) * 2 * N)
+            pairs = ps[:].rearrange("p a (i e) -> p (a i) e", e=2)
+            asl = slice(2 * c, 2 * c + 2)
+            nc.vector.scalar_tensor_tensor(
+                out=u[:, cols].rearrange("p (j e) -> p j e", e=2), in0=pairs, scalar=0.0,
+                in1=cosT[:, asl, :].rearrange("p a i -> p (a i)").unsqueeze(2).to_broadcast([P, 2 * NPAIR, 2]),
+                op0=ALU.max, op1=ALU.mult)
+            nc.vector.scalar_tensor_tensor(
+                out=w[:, cols].rearrange("p (j e) -> p j e", e=2), in0=pairs[:, :, ::-1], scalar=0.0,
+                in1=sinT[:, :, asl, :].rearrange("p e a i -> p (a i) e"),
+                op0=ALU.max, op1=ALU.mult)
+            if b == 0:
+                x_quant(2, 4, xgc)
+            for step in todo[:PER_BANK[b]]:
+                step()
+            todo = todo[PER_BANK[b]:]
+            nc.scalar.activation(out=xsp[:, cols], in_=ps[:].rearrange("p a n -> p (a n)"), func=ACT.Relu)
+            if b + 2 < 4 * NH:
+                mm(b + 2)
+            hb = slice(c * 2 * N, (c + 1) * 2 * N)
+            if alone:
+                adder = nc.vector if b == 4 * NH - 1 else nc.gpsimd
+                adder.tensor_tensor(out=qrt[:, cols], in0=u[:, cols], in1=w[:, cols], op=ALU.add)
+                nc.sync.dma_start(out=o0[:, hb], in_=xsp[:, cols])
+                nc.sync.dma_start(out=o1[:, hb], in_=qrt[:, cols])
+            elif cc == 1:
+                nc.gpsimd.tensor_tensor(out=qrt[:], in0=u[:], in1=w[:], op=ALU.add)
+                hc = slice((c - 1) * 2 * N, (c + 1) * 2 * N)
+                nc.sync.dma_start(out=o0[:, hc], in_=xsp[:])
+                nc.sync.dma_start(out=o1[:, hc], in_=qrt[:])

@@ -29,8 +29,8 @@ def tile_bdhlayer_pa_kernel(tc, x, encoder_bytes, encoder_scale, out_0, out_1):
     with ExitStack() as ctx:
         const = ctx.enter_context(tc.tile_pool(name="const", bufs=1))
         work = ctx.enter_context(tc.tile_pool(name="work", bufs=2))
-        outp = ctx.enter_context(tc.tile_pool(name="outp", bufs=4))
-        prod = ctx.enter_context(tc.tile_pool(name="prod", bufs=3))
+        outp = ctx.enter_context(tc.tile_pool(name="outp", bufs=12))
+        prod = ctx.enter_context(tc.tile_pool(name="prod", bufs=5))
         psm = ctx.enter_context(tc.psum_pool(name="psm", bufs=8))
 
         sc = const.tile([P, 4], F32, name="sc")
@@ -225,7 +225,7 @@ def tile_bdhlayer_pa_kernel(tc, x, encoder_bytes, encoder_scale, out_0, out_1):
             h, c = divmod(b, 4)
             o0 = out_0[0, h].rearrange("(p a) n -> p (a n)", a=TPP)
             o1 = out_1[0, h].rearrange("(p a) n -> p (a n)", a=TPP)
-            alone = b < 2 or b >= 4 * NH - 4
+            alone = b < 2 or b >= 4 * NH - 2
             cc = c % 2
             if cc == 0:
                 xsp = outp.tile([P, 4 * N], F32, name="xsp")
@@ -253,13 +253,12 @@ def tile_bdhlayer_pa_kernel(tc, x, encoder_bytes, encoder_scale, out_0, out_1):
             if b + 2 < 4 * NH:
                 mm(b + 2)
             hb = slice(c * 2 * N, (c + 1) * 2 * N)
+            adder = nc.vector if b == 4 * NH - 1 else nc.gpsimd
+            adder.tensor_tensor(out=qrt[:, cols], in0=u[:, cols], in1=w[:, cols], op=ALU.add)
             if alone:
-                adder = nc.vector if b == 4 * NH - 1 else nc.gpsimd
-                adder.tensor_tensor(out=qrt[:, cols], in0=u[:, cols], in1=w[:, cols], op=ALU.add)
                 nc.sync.dma_start(out=o0[:, hb], in_=xsp[:, cols])
                 nc.sync.dma_start(out=o1[:, hb], in_=qrt[:, cols])
             elif cc == 1:
-                nc.gpsimd.tensor_tensor(out=qrt[:], in0=u[:], in1=w[:], op=ALU.add)
                 hc = slice((c - 1) * 2 * N, (c + 1) * 2 * N)
                 nc.sync.dma_start(out=o0[:, hc], in_=xsp[:])
                 nc.sync.dma_start(out=o1[:, hc], in_=qrt[:])

@@ -57,6 +57,8 @@ def tile_bdhlayer_pa_kernel(tc, x, encoder_bytes, encoder_scale, out_0, out_1):
         load_enc(3)
         load_enc(4)
 
+        ctx.enter_context(tc.manual_schedule())
+
         warm = const.tile([P, 1], F32, name="warm")
         warm2 = const.tile([P, 1], F32, name="warm2")
         nc.vector.memset(warm[:], 0.0)
@@ -90,7 +92,7 @@ def tile_bdhlayer_pa_kernel(tc, x, encoder_bytes, encoder_scale, out_0, out_1):
             nc.vector.scalar_tensor_tensor(out=frac[:, a, :], in0=g[:], scalar=tcol[:, a:a + 1],
                                            in1=kint[:, a, :], op0=ALU.mult, op1=ALU.subtract)
 
-        def table_trig(a0, a1, neg_on_scalar):
+        def table_trig(a0, a1, neg_on_scalar, neg_on_gpsimd=True):
             sl = slice(a0, a1)
             nc.scalar.activation(out=sinT[:, 1, sl, :], in_=frac[:, sl, :], func=ACT.Sin, scale=TWO_PI)
             if neg_on_scalar:
@@ -98,7 +100,7 @@ def tile_bdhlayer_pa_kernel(tc, x, encoder_bytes, encoder_scale, out_0, out_1):
             nc.scalar.activation(out=afr[:, sl, :], in_=frac[:, sl, :], func=ACT.Abs)
             nc.scalar.activation(out=cosT[:, sl, :], in_=afr[:, sl, :], func=ACT.Sin,
                                  scale=-TWO_PI, bias=TWO_PI / 4.0)
-            if not neg_on_scalar:
+            if neg_on_gpsimd and not neg_on_scalar:
                 nc.gpsimd.tensor_scalar(out=sinT[:, 0, sl, :], in0=sinT[:, 1, sl, :], scalar1=-1.0,
                                         scalar2=0.0, op0=ALU.mult, op1=ALU.add)
 
@@ -213,22 +215,41 @@ def tile_bdhlayer_pa_kernel(tc, x, encoder_bytes, encoder_scale, out_0, out_1):
         mm(1)
         x_copy(2, nc.scalar.copy)
         x_copy(3, nc.scalar.copy)
-        table_trig(4, TPP, False)
+        table_trig(4, TPP, False, False)
 
         todo = []
         for gi in range(1, len(ENC_GROUPS)):
             todo.extend(enc_pieces(gi))
-        PER_BANK = (3, 3, 1, 2, 2, 2, 1, 2, 2, 2, 1, 3, 2, 2, 2) + (0,) * 9
+        PER_BANK = (3, 3, 3, 3, 0, 1, 1, 1, 3, 3, 1, 1, 1, 3, 3) + (0,) * 9
+        LAG = (0, 1, 2, 3) + (4,) * 10 + (3, 2, 1) + (0,) * 7
 
-        outs = {}
-        for b in range(4 * NH):
+        NB = 4 * NH
+        xsps = {}
+        relus = 0
+
+        def views(b):
             h, c = divmod(b, 4)
+            alone = b < 2 or b >= NB - 2
+            return h, c, alone
+
+        def relu(b):
+            h, c, alone = views(b)
             o0 = out_0[0, h].rearrange("(p a) n -> p (a n)", a=TPP)
+            if c % 2 == 0:
+                xsps[b // 2] = outp.tile([P, 4 * N], F32, name="xsp")
+            xsp = xsps[b // 2]
+            cols = slice((c % 2) * 2 * N, (c % 2 + 1) * 2 * N)
+            nc.scalar.activation(out=xsp[:, cols], in_=banks[b][:].rearrange("p a n -> p (a n)"), func=ACT.Relu)
+            if alone:
+                nc.sync.dma_start(out=o0[:, c * 2 * N:(c + 1) * 2 * N], in_=xsp[:, cols])
+            elif c % 2 == 1:
+                nc.sync.dma_start(out=o0[:, (c - 1) * 2 * N:(c + 1) * 2 * N], in_=xsp[:])
+
+        for b in range(NB):
+            h, c, alone = views(b)
             o1 = out_1[0, h].rearrange("(p a) n -> p (a n)", a=TPP)
-            alone = b < 2 or b >= 4 * NH - 2
             cc = c % 2
             if cc == 0:
-                xsp = outp.tile([P, 4 * N], F32, name="xsp")
                 qrt = outp.tile([P, 4 * N], F32, name="qrt")
                 u = prod.tile([P, 4 * N], F32, name="u")
                 w = prod.tile([P, 4 * N], F32, name="w")
@@ -246,19 +267,19 @@ def tile_bdhlayer_pa_kernel(tc, x, encoder_bytes, encoder_scale, out_0, out_1):
                 op0=ALU.max, op1=ALU.mult)
             if b == 0:
                 x_quant(2, 4, xgc)
+                nc.vector.tensor_scalar(out=sinT[:, 0, 4:TPP, :], in0=sinT[:, 1, 4:TPP, :], scalar1=-1.0,
+                                        scalar2=None, op0=ALU.mult)
             for step in todo[:PER_BANK[b]]:
                 step()
             todo = todo[PER_BANK[b]:]
-            nc.scalar.activation(out=xsp[:, cols], in_=ps[:].rearrange("p a n -> p (a n)"), func=ACT.Relu)
-            if b + 2 < 4 * NH:
+            while relus < b + 1 - LAG[b]:
+                relu(relus)
+                relus += 1
+            if b + 2 < NB:
                 mm(b + 2)
-            hb = slice(c * 2 * N, (c + 1) * 2 * N)
-            adder = nc.vector if b == 4 * NH - 1 else nc.gpsimd
+            adder = nc.vector if b == NB - 1 else nc.gpsimd
             adder.tensor_tensor(out=qrt[:, cols], in0=u[:, cols], in1=w[:, cols], op=ALU.add)
             if alone:
-                nc.sync.dma_start(out=o0[:, hb], in_=xsp[:, cols])
-                nc.sync.dma_start(out=o1[:, hb], in_=qrt[:, cols])
+                nc.sync.dma_start(out=o1[:, c * 2 * N:(c + 1) * 2 * N], in_=qrt[:, cols])
             elif cc == 1:
-                hc = slice((c - 1) * 2 * N, (c + 1) * 2 * N)
-                nc.sync.dma_start(out=o0[:, hc], in_=xsp[:])
-                nc.sync.dma_start(out=o1[:, hc], in_=qrt[:])
+                nc.sync.dma_start(out=o1[:, (c - 1) * 2 * N:(c + 1) * 2 * N], in_=qrt[:])

@@ -21,7 +21,7 @@ N = 256
 NPAIR = 128
 TPP = 8
 TWO_PI = 6.283185307179586
-ENC_GROUPS = ((0,), (1,), (2,), (3,), (4, 5))
+ENC_GROUPS = ((0,), (1,), (2,), (3,), (4,), (5,))
 
 
 def tile_bdhlayer_pa_kernel(tc, x, encoder_bytes, encoder_scale, out_0, out_1):
@@ -56,6 +56,7 @@ def tile_bdhlayer_pa_kernel(tc, x, encoder_bytes, encoder_scale, out_0, out_1):
         load_enc(2)
         load_enc(3)
         load_enc(4)
+        load_enc(5)
 
         ctx.enter_context(tc.manual_schedule())
 
@@ -150,9 +151,8 @@ def tile_bdhlayer_pa_kernel(tc, x, encoder_bytes, encoder_scale, out_0, out_1):
                     nc.scalar.activation(out=t_["ew"][:, t, :], in_=src[:, t, :].bitcast(FP8),
                                          func=ACT.Copy, scale=sc[:, t:t + 1])
 
-            def interleave(n0):
-                nc.scalar.copy(out=t_["eg"][:, n0:n0 + 128, :],
-                               in_=t_["ew"][:, :, n0:n0 + 128].rearrange("p t n -> p n t"))
+            def interleave():
+                nc.scalar.copy(out=t_["eg"][:], in_=t_["ew"][:].rearrange("p t n -> p n t"))
 
             def quantize():
                 nc.vector.quantize_mx(out=ec[gi][:].bitcast(FP8X4), scales=es[gi][:],
@@ -160,7 +160,7 @@ def tile_bdhlayer_pa_kernel(tc, x, encoder_bytes, encoder_scale, out_0, out_1):
 
             steps = [lambda t=t: widen(t) for t in range(4)]
             if gi > 0:
-                steps.extend([lambda n0=n0: interleave(n0) for n0 in range(0, wdt, 128)])
+                steps.append(interleave)
             steps.append(quantize)
             return steps
 
@@ -220,8 +220,8 @@ def tile_bdhlayer_pa_kernel(tc, x, encoder_bytes, encoder_scale, out_0, out_1):
         todo = []
         for gi in range(1, len(ENC_GROUPS)):
             todo.extend(enc_pieces(gi))
-        PER_BANK = (3, 3, 3, 3, 0, 1, 1, 1, 3, 3, 1, 1, 1, 3, 3) + (0,) * 9
-        LAG = (0, 1, 2, 3) + (4,) * 10 + (3, 2, 1) + (0,) * 7
+        PER_BANK = (3, 2, 1) + (2, 2, 1, 1) * 4 + (0,) * 5
+        LAG = (0,) * 18 + (-1,) + (-2,) * 5
 
         NB = 4 * NH
         xsps = {}
@@ -272,12 +272,12 @@ def tile_bdhlayer_pa_kernel(tc, x, encoder_bytes, encoder_scale, out_0, out_1):
             for step in todo[:PER_BANK[b]]:
                 step()
             todo = todo[PER_BANK[b]:]
-            while relus < b + 1 - LAG[b]:
-                relu(relus)
-                relus += 1
             if b + 2 < NB:
                 mm(b + 2)
-            adder = nc.vector if b == NB - 1 else nc.gpsimd
+            while relus < min(NB, b + 1 - LAG[b]):
+                relu(relus)
+                relus += 1
+            adder = nc.vector if b >= NB - 2 else nc.gpsimd
             adder.tensor_tensor(out=qrt[:, cols], in0=u[:, cols], in1=w[:, cols], op=ALU.add)
             if alone:
                 nc.sync.dma_start(out=o1[:, c * 2 * N:(c + 1) * 2 * N], in_=qrt[:, cols])

@@ -50,9 +50,9 @@ def tile_bdhlayer_pa_kernel(tc, x, encoder_bytes, encoder_scale, out_0, out_1):
         load_enc(0)
         load_x(0)
         load_x(1)
-        load_enc(1)
         load_x(2)
         load_x(3)
+        load_enc(1)
         load_enc(2)
         load_enc(3)
         load_enc(4)
@@ -68,16 +68,17 @@ def tile_bdhlayer_pa_kernel(tc, x, encoder_bytes, encoder_scale, out_0, out_1):
         tcol = const.tile([P, TPP], F32, name="tcol")
         nc.gpsimd.iota(tcol[:], pattern=[[1, TPP]], base=0, channel_multiplier=TPP,
                        allow_small_or_imprecise_dtypes=True)
+        expo = const.tile([P, 16], I32, name="expo")
+        nc.gpsimd.iota(expo[:], pattern=[[-1, 16]], base=127, channel_multiplier=0)
         ident = const.tile([P, P], F32, name="ident")
         make_identity(nc, ident[:])
 
+        pw = const.tile([P, 16], I32, name="pw")
+        nc.vector.tensor_scalar(out=pw[:], in0=expo[:], scalar1=23, scalar2=None, op0=ALU.logical_shift_left)
         g = const.tile([P, NPAIR], F32, name="g")
-        nc.vector.memset(g[:, 0:1], 1.0)
-        nc.vector.tensor_scalar(out=g[:, 0:1], in0=g[:, 0:1], scalar1=1.0 / TWO_PI, scalar2=None, op0=ALU.mult)
-        for b in range(7):
-            wd = 1 << b
-            nc.vector.tensor_scalar(out=g[:, wd:2 * wd], in0=g[:, 0:wd],
-                                    scalar1=2.0 ** (-wd / 8.0), scalar2=None, op0=ALU.mult)
+        for j in range(8):
+            nc.vector.tensor_scalar(out=g[:].rearrange("p (q j) -> p q j", j=8)[:, :, j], in0=pw[:].bitcast(F32),
+                                    scalar1=2.0 ** (-j / 8.0) / TWO_PI, scalar2=None, op0=ALU.mult)
 
         kint = const.tile([P, TPP, NPAIR], I32, name="kint")
         frac = const.tile([P, TPP, NPAIR], F32, name="frac")
@@ -171,7 +172,8 @@ def tile_bdhlayer_pa_kernel(tc, x, encoder_bytes, encoder_scale, out_0, out_1):
 
         xga = work.tile([P, 1024], BF16, name="xga", align_bytes=64)
         xgb = work.tile([P, 1024], BF16, name="xgb", align_bytes=64)
-        xgc = work.tile([P, 2048], BF16, name="xgc", align_bytes=64)
+        xgc = work.tile([P, 1024], BF16, name="xgc", align_bytes=64)
+        xgd = work.tile([P, 1024], BF16, name="xgd", align_bytes=64)
 
         banks = {}
 
@@ -188,40 +190,60 @@ def tile_bdhlayer_pa_kernel(tc, x, encoder_bytes, encoder_scale, out_0, out_1):
                                     start=True, stop=True)
             banks[b] = ps
 
-        for a in range(2):
+        def neg_sin(a0, a1, eng):
+            eng.tensor_scalar(out=sinT[:, 0, a0:a1, :], in0=sinT[:, 1, a0:a1, :], scalar1=-1.0,
+                              scalar2=0.0, op0=ALU.mult, op1=ALU.add)
+
+        for a in range(4):
             table_k(a, nc.vector)
+        for a in range(4):
             table_frac(a)
-        for a in range(2, TPP):
-            table_k(a, nc.gpsimd)
-        table_trig(0, 2, True)
-        table_frac(2)
-        table_frac(3)
-        table_trig(2, 4, False)
+        table_trig(0, 2, False, False)
+        neg_sin(0, 2, nc.gpsimd)
+        table_trig(2, 4, False, False)
+        neg_sin(2, 4, nc.gpsimd)
+        for a in range(4, TPP):
+            table_k(a, nc.vector)
         e0 = enc_pieces(0)
         for step in e0[:4]:
             step()
         x_transpose(0, xga, 0)
-        x_copy(0, nc.vector.tensor_copy)
-        for a in range(4, TPP):
-            table_frac(a)
+        x_copy(0, nc.scalar.copy)
+        table_frac(4)
+        table_frac(5)
         e0[4]()
         x_quant(0, 1, xga)
         x_transpose(1, xgb, 0)
-        x_transpose(2, xgc, 0)
-        x_transpose(3, xgc, 1024)
         x_copy(1, nc.scalar.copy)
+        x_transpose(2, xgc, 0)
+        x_transpose(3, xgd, 0)
         mm(0)
+        table_frac(6)
+        table_frac(7)
         x_quant(1, 2, xgb)
         mm(1)
+        table_trig(4, 6, False, False)
+        neg_sin(4, 6, nc.gpsimd)
         x_copy(2, nc.scalar.copy)
+        table_trig(6, TPP, False, False)
         x_copy(3, nc.scalar.copy)
-        table_trig(4, TPP, False, False)
 
-        todo = []
+        s_steps = {}
+        v_quant = {}
         for gi in range(1, len(ENC_GROUPS)):
-            todo.extend(enc_pieces(gi))
-        PER_BANK = (3, 2, 1) + (2, 2, 1, 1) * 4 + (0,) * 5
-        LAG = (0,) * 18 + (-1,) + (-2,) * 5
+            pieces = enc_pieces(gi)
+            s_steps[gi] = pieces[:5]
+            v_quant[gi] = pieces[5]
+        S_PLAN = {0: [(1, 0), (1, 1), (1, 2), (1, 3), (1, 4)]}
+        Q_PLAN = {2: 1}
+        for gi in range(2, len(ENC_GROUPS)):
+            S_PLAN[4 * gi - 5] = [(gi, 0), (gi, 1)]
+            S_PLAN[4 * gi - 4] = [(gi, 2), (gi, 3)]
+            S_PLAN[4 * gi - 3] = [(gi, 4)]
+            Q_PLAN[4 * gi - 2] = gi
+        RELUS = (0, 0, 0, 1, 2, 3, 5, 6, 7, 8, 10, 11, 12, 13, 15, 16, 17, 18, 20, 22, 23, 24, 24, 24)
+        AFTER = {0: [lambda: x_quant(2, 3, xgc), lambda: mm(2)],
+                 1: [lambda: neg_sin(6, TPP, nc.vector), lambda: x_quant(3, 4, xgd), lambda: mm(3)]}
 
         NB = 4 * NH
         xsps = {}
@@ -265,16 +287,15 @@ def tile_bdhlayer_pa_kernel(tc, x, encoder_bytes, encoder_scale, out_0, out_1):
                 out=w[:, cols].rearrange("p (j e) -> p j e", e=2), in0=pairs[:, :, ::-1], scalar=0.0,
                 in1=sinT[:, :, asl, :].rearrange("p e a i -> p (a i) e"),
                 op0=ALU.max, op1=ALU.mult)
-            if b == 0:
-                x_quant(2, 4, xgc)
-                nc.vector.tensor_scalar(out=sinT[:, 0, 4:TPP, :], in0=sinT[:, 1, 4:TPP, :], scalar1=-1.0,
-                                        scalar2=None, op0=ALU.mult)
-            for step in todo[:PER_BANK[b]]:
+            for step in AFTER.get(b, []):
                 step()
-            todo = todo[PER_BANK[b]:]
-            if b + 2 < NB:
+            for gi, k in S_PLAN.get(b, []):
+                s_steps[gi][k]()
+            if b in Q_PLAN:
+                v_quant[Q_PLAN[b]]()
+            if 2 <= b and b + 2 < NB:
                 mm(b + 2)
-            while relus < min(NB, b + 1 - LAG[b]):
+            while relus < RELUS[b]:
                 relu(relus)
                 relus += 1
             adder = nc.vector if b >= NB - 2 else nc.gpsimd

@@ -267,9 +267,25 @@ def tile_bdhlayer_pa_kernel(tc, x, encoder_bytes, encoder_scale, out_0, out_1):
             elif c % 2 == 1:
                 nc.sync.dma_start(out=o0[:, (c - 1) * 2 * N:(c + 1) * 2 * N], in_=xsp[:])
 
-        for b in range(NB):
+        V_ADD = (13,)
+        parts = {}
+        written = {}
+
+        def add_and_store(b, eng):
             h, c, alone = views(b)
             o1 = out_1[0, h].rearrange("(p a) n -> p (a n)", a=TPP)
+            qrt, u, w, cols = parts[b]
+            eng.tensor_tensor(out=qrt[:, cols], in0=u[:, cols], in1=w[:, cols], op=ALU.add)
+            if alone:
+                nc.sync.dma_start(out=o1[:, c * 2 * N:(c + 1) * 2 * N], in_=qrt[:, cols])
+                return
+            written[b // 2] = written.get(b // 2, 0) + 1
+            if written[b // 2] == 2:
+                c0 = c - c % 2
+                nc.sync.dma_start(out=o1[:, c0 * 2 * N:(c0 + 2) * 2 * N], in_=qrt[:])
+
+        for b in range(NB):
+            h, c, alone = views(b)
             cc = c % 2
             if cc == 0:
                 qrt = outp.tile([P, 4 * N], F32, name="qrt")
@@ -283,6 +299,8 @@ def tile_bdhlayer_pa_kernel(tc, x, encoder_bytes, encoder_scale, out_0, out_1):
                 out=u[:, cols].rearrange("p (j e) -> p j e", e=2), in0=pairs, scalar=0.0,
                 in1=cosT[:, asl, :].rearrange("p a i -> p (a i)").unsqueeze(2).to_broadcast([P, 2 * NPAIR, 2]),
                 op0=ALU.max, op1=ALU.mult)
+            if b - 1 in V_ADD:
+                add_and_store(b - 1, nc.vector)
             nc.vector.scalar_tensor_tensor(
                 out=w[:, cols].rearrange("p (j e) -> p j e", e=2), in0=pairs[:, :, ::-1], scalar=0.0,
                 in1=sinT[:, :, asl, :].rearrange("p e a i -> p (a i) e"),
@@ -298,9 +316,6 @@ def tile_bdhlayer_pa_kernel(tc, x, encoder_bytes, encoder_scale, out_0, out_1):
             while relus < RELUS[b]:
                 relu(relus)
                 relus += 1
-            adder = nc.vector if b >= NB - 2 else nc.gpsimd
-            adder.tensor_tensor(out=qrt[:, cols], in0=u[:, cols], in1=w[:, cols], op=ALU.add)
-            if alone:
-                nc.sync.dma_start(out=o1[:, c * 2 * N:(c + 1) * 2 * N], in_=qrt[:, cols])
-            elif cc == 1:
-                nc.sync.dma_start(out=o1[:, (c - 1) * 2 * N:(c + 1) * 2 * N], in_=qrt[:])
+            parts[b] = (qrt, u, w, cols)
+            if b not in V_ADD:
+                add_and_store(b, nc.vector if b >= NB - 2 else nc.gpsimd)

@@ -96,10 +96,10 @@ def tile_bdhlayer_pa_kernel(tc, x, encoder_bytes, encoder_scale, out_0, out_1):
 
         def table_trig(a0, a1, neg_on_scalar, neg_on_gpsimd=True):
             sl = slice(a0, a1)
+            nc.scalar.activation(out=afr[:, sl, :], in_=frac[:, sl, :], func=ACT.Abs)
             nc.scalar.activation(out=sinT[:, 1, sl, :], in_=frac[:, sl, :], func=ACT.Sin, scale=TWO_PI)
             if neg_on_scalar:
                 nc.scalar.activation(out=sinT[:, 0, sl, :], in_=frac[:, sl, :], func=ACT.Sin, scale=-TWO_PI)
-            nc.scalar.activation(out=afr[:, sl, :], in_=frac[:, sl, :], func=ACT.Abs)
             nc.scalar.activation(out=cosT[:, sl, :], in_=afr[:, sl, :], func=ACT.Sin,
                                  scale=-TWO_PI, bias=TWO_PI / 4.0)
             if neg_on_gpsimd and not neg_on_scalar:
@@ -153,7 +153,8 @@ def tile_bdhlayer_pa_kernel(tc, x, encoder_bytes, encoder_scale, out_0, out_1):
                                          func=ACT.Copy, scale=sc[:, t:t + 1])
 
             def interleave():
-                nc.scalar.copy(out=t_["eg"][:], in_=t_["ew"][:].rearrange("p t n -> p n t"))
+                nc.scalar.copy(out=t_["eg"][:].rearrange("p (c i) t -> p c t i", i=4),
+                               in_=t_["ew"][:].rearrange("p t (c i) -> p c t i", i=4))
 
             def quantize():
                 nc.vector.quantize_mx(out=ec[gi][:].bitcast(FP8X4), scales=es[gi][:],
@@ -216,8 +217,8 @@ def tile_bdhlayer_pa_kernel(tc, x, encoder_bytes, encoder_scale, out_0, out_1):
         x_transpose(1, xgb, 0)
         x_copy(1, nc.scalar.copy)
         x_transpose(2, xgc, 0)
-        x_transpose(3, xgd, 0)
         mm(0)
+        x_transpose(3, xgd, 0)
         table_frac(6)
         table_frac(7)
         x_quant(1, 2, xgb)

@@ -226,7 +226,8 @@ def tile_bdhlayer_pa_kernel(tc, x, encoder_bytes, encoder_scale, out_0, out_1):
         table_trig(4, 6, False, False)
         neg_sin(4, 6, nc.gpsimd)
         x_copy(2, nc.scalar.copy)
-        table_trig(6, TPP, False, False)
+        nc.scalar.activation(out=afr[:, 6:TPP, :], in_=frac[:, 6:TPP, :], func=ACT.Abs)
+        nc.scalar.activation(out=sinT[:, 1, 6:TPP, :], in_=frac[:, 6:TPP, :], func=ACT.Sin, scale=TWO_PI)
         x_copy(3, nc.scalar.copy)
 
         s_steps = {}
@@ -235,19 +236,24 @@ def tile_bdhlayer_pa_kernel(tc, x, encoder_bytes, encoder_scale, out_0, out_1):
             pieces = enc_pieces(gi)
             s_steps[gi] = pieces[:5]
             v_quant[gi] = pieces[5]
-        S_PLAN = {0: [(1, 0), (1, 1), (1, 2), (1, 3), (1, 4)]}
+        for k in range(4):
+            s_steps[1][k]()
+        nc.scalar.activation(out=cosT[:, 6:TPP, :], in_=afr[:, 6:TPP, :], func=ACT.Sin,
+                             scale=-TWO_PI, bias=TWO_PI / 4.0)
+        S_PLAN = {0: [(1, 4)]}
         Q_PLAN = {2: 1}
         for gi in range(2, len(ENC_GROUPS)):
             S_PLAN[4 * gi - 5] = [(gi, 0), (gi, 1)]
             S_PLAN[4 * gi - 4] = [(gi, 2), (gi, 3)]
             S_PLAN[4 * gi - 3] = [(gi, 4)]
             Q_PLAN[4 * gi - 2] = gi
-        RELUS = (0, 0, 0, 1, 2, 3, 5, 6, 7, 8, 10, 11, 12, 13, 15, 16, 17, 18, 20, 22, 23, 24, 24, 24)
+        RELU_AT = ((), (), (), (0,), (1,), (2,), (3, 4), (5,), (6,), (7,), (8, 9), (10,), (11,), (12,), (13, 14), (15,), (16,), (17,), (18,), (19, 21), (20, 22), (23,), (), ())
         AFTER = {0: [lambda: x_quant(2, 3, xgc), lambda: mm(2)],
                  1: [lambda: neg_sin(6, TPP, nc.vector), lambda: x_quant(3, 4, xgd), lambda: mm(3)]}
 
         NB = 4 * NH
         xsps = {}
+        half_done = set()
         relus = 0
 
         def views(b):
@@ -258,17 +264,20 @@ def tile_bdhlayer_pa_kernel(tc, x, encoder_bytes, encoder_scale, out_0, out_1):
         def relu(b):
             h, c, alone = views(b)
             o0 = out_0[0, h].rearrange("(p a) n -> p (a n)", a=TPP)
-            if c % 2 == 0:
+            if b // 2 not in xsps:
                 xsps[b // 2] = outp.tile([P, 4 * N], F32, name="xsp")
             xsp = xsps[b // 2]
             cols = slice((c % 2) * 2 * N, (c % 2 + 1) * 2 * N)
             nc.scalar.activation(out=xsp[:, cols], in_=banks[b][:].rearrange("p a n -> p (a n)"), func=ACT.Relu)
             if alone:
                 nc.sync.dma_start(out=o0[:, c * 2 * N:(c + 1) * 2 * N], in_=xsp[:, cols])
-            elif c % 2 == 1:
-                nc.sync.dma_start(out=o0[:, (c - 1) * 2 * N:(c + 1) * 2 * N], in_=xsp[:])
+            elif b // 2 in half_done:
+                c0 = c - c % 2
+                nc.sync.dma_start(out=o0[:, c0 * 2 * N:(c0 + 2) * 2 * N], in_=xsp[:])
+            else:
+                half_done.add(b // 2)
 
-        V_ADD = (13,)
+        V_ADD = (13, 22)
         parts = {}
         written = {}
 
@@ -314,9 +323,8 @@ def tile_bdhlayer_pa_kernel(tc, x, encoder_bytes, encoder_scale, out_0, out_1):
                 v_quant[Q_PLAN[b]]()
             if 2 <= b and b + 2 < NB:
                 mm(b + 2)
-            while relus < RELUS[b]:
-                relu(relus)
-                relus += 1
+            for r in RELU_AT[b]:
+                relu(r)
             parts[b] = (qrt, u, w, cols)
             if b not in V_ADD:
-                add_and_store(b, nc.vector if b >= NB - 2 else nc.gpsimd)
+                add_and_store(b, nc.vector if b == NB - 1 else nc.gpsimd)

from contextlib import ExitStack

import concourse.mybir as mybir
from concourse.masks import make_identity

FLOPS = 2 * 1024 * 512 * 1536

F32 = mybir.dt.float32
BF16 = mybir.dt.bfloat16
I32 = mybir.dt.int32
U32 = mybir.dt.uint32
U8 = mybir.dt.uint8
FP8 = mybir.dt.float8_e4m3fn
FP8X4 = mybir.dt.float8_e4m3fn_x4
ALU = mybir.AluOpType
ACT = mybir.ActivationFunctionType

P = 128
NH = 6
N = 256
NPAIR = 128
TPP = 8
TWO_PI = 6.283185307179586
ENC_GROUPS = ((0,), (1,), (2,), (3,), (4,), (5,))


def tile_bdhlayer_pa_kernel(tc, x, encoder_bytes, encoder_scale, out_0, out_1):
    nc = tc.nc
    with ExitStack() as ctx:
        const = ctx.enter_context(tc.tile_pool(name="const", bufs=1))
        work = ctx.enter_context(tc.tile_pool(name="work", bufs=2))
        outp = ctx.enter_context(tc.tile_pool(name="outp", bufs=12))
        prod = ctx.enter_context(tc.tile_pool(name="prod", bufs=5))
        psm = ctx.enter_context(tc.psum_pool(name="psm", bufs=8))

        sc = const.tile([P, 4], F32, name="sc")
        nc.sync.dma_start(out=sc[:], in_=encoder_scale.rearrange("o (p t) u -> p (o t u)", t=4))
        eb = [const.tile([P, 4, len(grp), N], U8, name="eb%d" % gi) for gi, grp in enumerate(ENC_GROUPS)]
        xin = [const.tile([P, 2, 512], BF16, name="xin%d" % c) for c in range(4)]
        xr = x.rearrange("b o (p a) k -> p (b o a) k", a=TPP)

        def load_enc(gi):
            for s, h in enumerate(ENC_GROUPS[gi]):
                nc.sync.dma_start(out=eb[gi][:, :, s, :],
                                  in_=encoder_bytes[h].rearrange("(p t) n -> p t n", t=4))

        def load_x(c):
            nc.sync.dma_start(out=xin[c][:], in_=xr[:, 2 * c:2 * c + 2, :])

        load_enc(0)
        load_x(0)
        load_x(1)
        load_x(2)
        load_x(3)
        load_enc(1)
        load_enc(2)
        load_enc(3)
        load_enc(4)
        load_enc(5)

        ctx.enter_context(tc.manual_schedule())

        warm = const.tile([P, 1], F32, name="warm")
        warm2 = const.tile([P, 1], F32, name="warm2")
        nc.vector.memset(warm[:], 0.0)
        nc.scalar.activation(out=warm2[:], in_=warm[:], func=ACT.Sin)

        tcol = const.tile([P, TPP], F32, name="tcol")
        nc.gpsimd.iota(tcol[:], pattern=[[1, TPP]], base=0, channel_multiplier=TPP,
                       allow_small_or_imprecise_dtypes=True)
        expo = const.tile([P, 16], I32, name="expo")
        nc.gpsimd.iota(expo[:], pattern=[[-1, 16]], base=127, channel_multiplier=0)
        ident = const.tile([P, P], F32, name="ident")
        make_identity(nc, ident[:])

        pw = const.tile([P, 16], I32, name="pw")
        nc.vector.tensor_scalar(out=pw[:], in0=expo[:], scalar1=23, scalar2=None, op0=ALU.logical_shift_left)
        g = const.tile([P, NPAIR], F32, name="g")
        for j in range(8):
            nc.vector.tensor_scalar(out=g[:].rearrange("p (q j) -> p q j", j=8)[:, :, j], in0=pw[:].bitcast(F32),
                                    scalar1=2.0 ** (-j / 8.0) / TWO_PI, scalar2=None, op0=ALU.mult)

        kint = const.tile([P, TPP, NPAIR], I32, name="kint")
        frac = const.tile([P, TPP, NPAIR], F32, name="frac")
        afr = const.tile([P, TPP, NPAIR], F32, name="afr")
        cosT = const.tile([P, TPP, NPAIR], F32, name="cosT")
        sinT = const.tile([P, 2, TPP, NPAIR], F32, name="sinT")

        def table_k(a, eng):
            eng.tensor_scalar(out=kint[:, a, :], in0=g[:], scalar1=tcol[:, a:a + 1],
                              scalar2=0.0, op0=ALU.mult, op1=ALU.add)

        def table_frac(a):
            nc.vector.scalar_tensor_tensor(out=frac[:, a, :], in0=g[:], scalar=tcol[:, a:a + 1],
                                           in1=kint[:, a, :], op0=ALU.mult, op1=ALU.subtract)

        def table_trig(a0, a1, neg_on_scalar, neg_on_gpsimd=True):
            sl = slice(a0, a1)
            nc.scalar.activation(out=afr[:, sl, :], in_=frac[:, sl, :], func=ACT.Abs)
            nc.scalar.activation(out=sinT[:, 1, sl, :], in_=frac[:, sl, :], func=ACT.Sin, scale=TWO_PI)
            if neg_on_scalar:
                nc.scalar.activation(out=sinT[:, 0, sl, :], in_=frac[:, sl, :], func=ACT.Sin, scale=-TWO_PI)
            nc.scalar.activation(out=cosT[:, sl, :], in_=afr[:, sl, :], func=ACT.Sin,
                                 scale=-TWO_PI, bias=TWO_PI / 4.0)
            if neg_on_gpsimd and not neg_on_scalar:
                nc.gpsimd.tensor_scalar(out=sinT[:, 0, sl, :], in0=sinT[:, 1, sl, :], scalar1=-1.0,
                                        scalar2=0.0, op0=ALU.mult, op1=ALU.add)

        xc = const.tile([P, TPP * P], U32, name="xc", align_bytes=64)
        xs = const.tile([P, TPP * P], U8, name="xs", align_bytes=64)

        xg = [None, None, None, None]

        def x_transpose(c, tile_, col0):
            xt = psm.tile([P, 2, 2, P], F32, name="ps")
            for j in range(2):
                words = xin[c][:, j, :].bitcast(F32)
                for u in range(2):
                    nc.tensor.transpose(xt[:, j, u, :], words[:, u:256:2], ident[:])
            xg[c] = (xt, tile_, col0)

        def x_copy(c, copier):
            xt, tile_, col0 = xg[c]
            copier(out=tile_[:, col0:col0 + 1024].bitcast(F32).rearrange("p (a r u) -> p a r u", a=2, u=2),
                   in_=xt[:].rearrange("p a u r -> p a r u"))

        def x_quant(c0, c1, tile_):
            cols = slice(c0 * 2 * P, c1 * 2 * P)
            nc.vector.quantize_mx(out=xc[:, cols].bitcast(FP8X4), scales=xs[:, cols], in_=tile_[:])

        ec = [const.tile([P, len(grp) * N], U32, name="ec%d" % gi, align_bytes=64) for gi, grp in enumerate(ENC_GROUPS)]
        es = [const.tile([P, len(grp) * N], U8, name="es%d" % gi, align_bytes=64) for gi, grp in enumerate(ENC_GROUPS)]
        where = {}
        for gi, grp in enumerate(ENC_GROUPS):
            for s, h in enumerate(grp):
                where[h] = (gi, s)

        def enc_pieces(gi):
            wdt = len(ENC_GROUPS[gi]) * N
            src = eb[gi][:].rearrange("p t s n -> p t (s n)")
            t_ = {}

            def widen(t):
                if t == 0:
                    t_["eg"] = work.tile([P, wdt, 4], BF16, name="eg%d" % wdt, align_bytes=64)
                    if gi > 0:
                        t_["ew"] = work.tile([P, 4, wdt], BF16, name="ew%d" % wdt)
                if gi == 0:
                    nc.vector.tensor_scalar(out=t_["eg"][:, :, t], in0=src[:, t, :].bitcast(FP8),
                                            scalar1=sc[:, t:t + 1], scalar2=None, op0=ALU.mult)
                else:
                    nc.scalar.activation(out=t_["ew"][:, t, :], in_=src[:, t, :].bitcast(FP8),
                                         func=ACT.Copy, scale=sc[:, t:t + 1])

            def interleave():
                nc.scalar.copy(out=t_["eg"][:].rearrange("p (c i) t -> p c t i", i=4),
                               in_=t_["ew"][:].rearrange("p t (c i) -> p c t i", i=4))

            def quantize():
                nc.vector.quantize_mx(out=ec[gi][:].bitcast(FP8X4), scales=es[gi][:],
                                      in_=t_["eg"][:].rearrange("p n t -> p (n t)"))

            steps = [lambda t=t: widen(t) for t in range(4)]
            if gi > 0:
                steps.append(interleave)
            steps.append(quantize)
            return steps

        def prep_enc(gi):
            for step in enc_pieces(gi):
                step()


        xga = work.tile([P, 1024], BF16, name="xga", align_bytes=64)
        xgb = work.tile([P, 1024], BF16, name="xgb", align_bytes=64)
        xgc = work.tile([P, 1024], BF16, name="xgc", align_bytes=64)
        xgd = work.tile([P, 1024], BF16, name="xgd", align_bytes=64)

        banks = {}

        def mm(b):
            h, c = divmod(b, 4)
            gi, s = where[h]
            ps = psm.tile([P, 2, N], F32, name="ps")
            for j in range(2):
                tok = slice((2 * c + j) * P, (2 * c + j + 1) * P)
                nc.tensor.matmul_mx(out=ps[:, j, :],
                                    lhsT=xc[:, tok].bitcast(FP8X4), lhsT_scale=xs[:, tok],
                                    rhs=ec[gi][:, s * N:(s + 1) * N].bitcast(FP8X4),
                                    rhs_scale=es[gi][:, s * N:(s + 1) * N],
                                    start=True, stop=True)
            banks[b] = ps

        def neg_sin(a0, a1, eng):
            eng.tensor_scalar(out=sinT[:, 0, a0:a1, :], in0=sinT[:, 1, a0:a1, :], scalar1=-1.0,
                              scalar2=0.0, op0=ALU.mult, op1=ALU.add)

        for a in range(4):
            table_k(a, nc.vector)
        for a in range(4):
            table_frac(a)
        table_trig(0, 2, False, False)
        neg_sin(0, 2, nc.gpsimd)
        table_trig(2, 4, False, False)
        neg_sin(2, 4, nc.gpsimd)
        for a in range(4, TPP):
            table_k(a, nc.vector)
        e0 = enc_pieces(0)
        for step in e0[:4]:
            step()
        x_transpose(0, xga, 0)
        x_copy(0, nc.scalar.copy)
        table_frac(4)
        table_frac(5)
        e0[4]()
        x_quant(0, 1, xga)
        x_transpose(1, xgb, 0)
        x_copy(1, nc.scalar.copy)
        x_transpose(2, xgc, 0)
        mm(0)
        x_transpose(3, xgd, 0)
        table_frac(6)
        table_frac(7)
        x_quant(1, 2, xgb)
        mm(1)
        table_trig(4, 6, False, False)
        neg_sin(4, 6, nc.gpsimd)
        x_copy(2, nc.scalar.copy)
        nc.scalar.activation(out=afr[:, 6:TPP, :], in_=frac[:, 6:TPP, :], func=ACT.Abs)
        nc.scalar.activation(out=sinT[:, 1, 6:TPP, :], in_=frac[:, 6:TPP, :], func=ACT.Sin, scale=TWO_PI)
        x_copy(3, nc.scalar.copy)

        s_steps = {}
        v_quant = {}
        for gi in range(1, len(ENC_GROUPS)):
            pieces = enc_pieces(gi)
            s_steps[gi] = pieces[:5]
            v_quant[gi] = pieces[5]
        for k in range(4):
            s_steps[1][k]()
        nc.scalar.activation(out=cosT[:, 6:TPP, :], in_=afr[:, 6:TPP, :], func=ACT.Sin,
                             scale=-TWO_PI, bias=TWO_PI / 4.0)
        S_PLAN = {0: [(1, 4)]}
        Q_PLAN = {2: 1}
        for gi in range(2, len(ENC_GROUPS)):
            S_PLAN[4 * gi - 5] = [(gi, 0), (gi, 1)]
            S_PLAN[4 * gi - 4] = [(gi, 2), (gi, 3)]
            S_PLAN[4 * gi - 3] = [(gi, 4)]
            Q_PLAN[4 * gi - 2] = gi
        RELU_AT = ((), (), (), (0,), (1,), (2,), (3, 4), (5,), (6,), (7,), (8, 9), (10,), (11,), (12,), (13, 14), (15,), (16,), (17,), (18,), (19, 21), (20, 22), (23,), (), ())
        AFTER = {0: [lambda: x_quant(2, 3, xgc), lambda: mm(2)],
                 1: [lambda: neg_sin(6, TPP, nc.vector), lambda: x_quant(3, 4, xgd), lambda: mm(3)]}

        NB = 4 * NH
        xsps = {}
        half_done = set()
        relus = 0

        def views(b):
            h, c = divmod(b, 4)
            alone = b < 2 or b >= NB - 2
            return h, c, alone

        def relu(b):
            h, c, alone = views(b)
            o0 = out_0[0, h].rearrange("(p a) n -> p (a n)", a=TPP)
            if b // 2 not in xsps:
                xsps[b // 2] = outp.tile([P, 4 * N], F32, name="xsp")
            xsp = xsps[b // 2]
            cols = slice((c % 2) * 2 * N, (c % 2 + 1) * 2 * N)
            nc.scalar.activation(out=xsp[:, cols], in_=banks[b][:].rearrange("p a n -> p (a n)"), func=ACT.Relu)
            if alone:
                nc.sync.dma_start(out=o0[:, c * 2 * N:(c + 1) * 2 * N], in_=xsp[:, cols])
            elif b // 2 in half_done:
                c0 = c - c % 2
                nc.sync.dma_start(out=o0[:, c0 * 2 * N:(c0 + 2) * 2 * N], in_=xsp[:])
            else:
                half_done.add(b // 2)

        V_ADD = (13, 22)
        parts = {}
        written = {}

        def add_and_store(b, eng):
            h, c, alone = views(b)
            o1 = out_1[0, h].rearrange("(p a) n -> p (a n)", a=TPP)
            qrt, u, w, cols = parts[b]
            eng.tensor_tensor(out=qrt[:, cols], in0=u[:, cols], in1=w[:, cols], op=ALU.add)
            if alone:
                nc.sync.dma_start(out=o1[:, c * 2 * N:(c + 1) * 2 * N], in_=qrt[:, cols])
                return
            written[b // 2] = written.get(b // 2, 0) + 1
            if written[b // 2] == 2:
                c0 = c - c % 2
                nc.sync.dma_start(out=o1[:, c0 * 2 * N:(c0 + 2) * 2 * N], in_=qrt[:])

        for b in range(NB):
            h, c, alone = views(b)
            cc = c % 2
            if cc == 0:
                qrt = outp.tile([P, 4 * N], F32, name="qrt")
                u = prod.tile([P, 4 * N], F32, name="u")
                w = prod.tile([P, 4 * N], F32, name="w")
            ps = banks[b]
            cols = slice(cc * 2 * N, (cc + 1) * 2 * N)
            pairs = ps[:].rearrange("p a (i e) -> p (a i) e", e=2)
            asl = slice(2 * c, 2 * c + 2)
            nc.vector.scalar_tensor_tensor(
                out=u[:, cols].rearrange("p (j e) -> p j e", e=2), in0=pairs, scalar=0.0,
                in1=cosT[:, asl, :].rearrange("p a i -> p (a i)").unsqueeze(2).to_broadcast([P, 2 * NPAIR, 2]),
                op0=ALU.max, op1=ALU.mult)
            if b - 1 in V_ADD:
                add_and_store(b - 1, nc.vector)
            nc.vector.scalar_tensor_tensor(
                out=w[:, cols].rearrange("p (j e) -> p j e", e=2), in0=pairs[:, :, ::-1], scalar=0.0,
                in1=sinT[:, :, asl, :].rearrange("p e a i -> p (a i) e"),
                op0=ALU.max, op1=ALU.mult)
            for step in AFTER.get(b, []):
                step()
            for gi, k in S_PLAN.get(b, []):
                s_steps[gi][k]()
            if b in Q_PLAN:
                v_quant[Q_PLAN[b]]()
            if 2 <= b and b + 2 < NB:
                mm(b + 2)
            for r in RELU_AT[b]:
                relu(r)
            parts[b] = (qrt, u, w, cols)
            if b not in V_ADD:
                add_and_store(b, nc.vector if b == NB - 1 else nc.gpsimd)
